import numpy as np
import ml_dtypes


def mxq(x, axis, fmt="e4m3"):
    dtype, down = {"e4m3": (ml_dtypes.float8_e4m3fn, 7), "e5m2": (ml_dtypes.float8_e5m2, 14)}[fmt]
    v = np.moveaxis(np.asarray(x, np.float32).astype(ml_dtypes.bfloat16).astype(np.float64), axis, -1)
    blocks = v.reshape(v.shape[:-1] + (-1, 32))
    amax = np.abs(blocks).max(-1, keepdims=True)
    byte = np.maximum(np.where(amax > 0, np.frexp(amax)[1] - 1 + 127, 0) - down, 1)
    scale = np.exp2(byte - 127.0)
    codes = (blocks / scale).astype(np.float32).astype(dtype).astype(np.float64)
    return np.moveaxis((codes * scale).reshape(v.shape), -1, axis)


WIDE = False


def mx_kscale(k):
    if not WIDE:
        return np.ones(k)
    levels = np.array([10, -10, 5, -5, 0])
    a = np.random.permutation(np.resize(levels, k // 512 * 4)).reshape(k // 512, 4)
    idx = np.arange(k)
    return np.exp2(a[idx // 512, idx % 128 // 32])


BF16 = ml_dtypes.bfloat16


def bf(x):
    return np.asarray(x, np.float32).astype(BF16)


def f64(x):
    return np.asarray(x).astype(np.float64)


H, N, S, T, L, K = 2, 2, 1024, 1024, 2048, 1024
NH = N * H


def rel_shift(p):
    zero_pad = np.zeros((NH, S, 1))
    padded = np.concatenate([zero_pad, p], axis=2)
    padded = padded.reshape(NH, T + 1, S)
    return padded[:, 1:, :].reshape(NH, S, T)


def setup_inputs():
    s = mx_kscale(K)
    return {"queries": bf(np.random.standard_normal((NH, S, K)) * s),
            "v_bias": bf(np.random.standard_normal((1, H, 1, K)) / np.sqrt(K) * s),
            "R": bf(np.random.standard_normal((H, L, K)) / s)}


def reference(queries, v_bias, R):
    q = (f64(queries) * K ** -0.5).reshape(N, H, S, K)
    q_v = q + f64(v_bias)
    r = f64(R)[:, :T, :]
    pos = mxq(q_v, 3, "e4m3") @ mxq(r, 2, "e4m3").transpose(0, 2, 1)
    return rel_shift(pos.reshape(NH, S, T))

@@ -1,0 +1,199 @@
+from contextlib import ExitStack
+
+import concourse.mybir as mybir
+from concourse.masks import make_identity
+
+BF16 = mybir.dt.bfloat16
+F32 = mybir.dt.float32
+U32 = mybir.dt.uint32
+U8 = mybir.dt.uint8
+FP8X4 = mybir.dt.float8_e4m3fn_x4
+
+P = 128
+HEADS = 2
+BATCH = 4
+S = 1024
+T = 1024
+K = 1024
+K_PASS = 4 * P
+PASSES = K // K_PASS
+WORDS = K // 2
+CHUNK_TILES = 4
+CHUNK_ROWS = CHUNK_TILES * P
+HALVES = S // CHUNK_ROWS
+N_COLS = CHUNK_ROWS
+ROWS_EACH = S // P
+PADDED = T + 1
+RUN = ROWS_EACH * PADDED
+ROOT_K = 32.0
+assert ROOT_K * ROOT_K == K
+
+FLOPS = 2 * BATCH * S * T * K
+BYTES = 2 * BATCH * S * K + 2 * HEADS * K + 2 * HEADS * T * K + 4 * BATCH * S * T
+
+
+def skewed_rows(out_flat, first, rows, width):
+    lead = min(first, RUN - width)
+    window = out_flat[first - lead : first - lead + rows * RUN]
+    return window.rearrange("(r x) -> r x", x=RUN)[:, lead : lead + width]
+
+
+def tile_relativepositionsdpa_pa_t_kernel(tc, queries, v_bias, R, out):
+    nc = tc.nc
+    out_flat = out.rearrange("b s t -> (b s t)")
+
+    with ExitStack() as ctx:
+        consts = ctx.enter_context(tc.tile_pool(name="consts", bufs=1))
+        raws = ctx.enter_context(tc.tile_pool(name="raws", bufs=6))
+        groupeds = ctx.enter_context(tc.tile_pool(name="groupeds", bufs=3))
+        tables = ctx.enter_context(tc.tile_pool(name="tables", bufs=1))
+        operands = ctx.enter_context(tc.tile_pool(name="operands", bufs=3))
+        results = ctx.enter_context(tc.tile_pool(name="results", bufs=3))
+        banks = ctx.enter_context(tc.psum_pool(name="banks", bufs=4))
+        sums = ctx.enter_context(tc.psum_pool(name="sums", bufs=4))
+
+        def load_chunk(rows, name):
+            raw = raws.tile([P, CHUNK_TILES * K], BF16, name=name, tag="raw")
+            nc.sync.dma_start(out=raw[:].rearrange("p (t k) -> p t k", t=CHUNK_TILES), in_=rows)
+            return raw
+
+        v_rows = consts.tile([P, 2 * P], BF16, name="v_rows")
+        nc.vector.memset(v_rows[:], 0.0)
+
+        raw_queries = {}
+        raw_tables = {}
+        for b in range(BATCH):
+            rows_of_b = queries[b].rearrange("(p t) k -> p t k", t=ROWS_EACH)
+            for half in range(HALVES):
+                tiles = slice(half * CHUNK_TILES, (half + 1) * CHUNK_TILES)
+                raw_queries[b, half] = load_chunk(rows_of_b[:, tiles, :], "raw_q%d%d" % (b, half))
+                if half == 0 and b == 0:
+                    nc.sync.dma_start(
+                        out=v_rows[0 : 2 * PASSES * HEADS, :],
+                        in_=v_bias.rearrange("a h c (r w) -> (a h c r) w", w=2 * P),
+                    )
+                if half == 0 and b < HEADS:
+                    for n in range(HALVES):
+                        rows = R[b, n * CHUNK_ROWS : (n + 1) * CHUNK_ROWS, :]
+                        raw_tables[b, n] = load_chunk(
+                            rows.rearrange("(t p) k -> p t k", p=P), "raw_r%d%d" % (b, n)
+                        )
+
+        ident = consts.tile([P, P], F32, name="ident")
+        make_identity(nc, ident[:])
+        zeros = consts.tile([P, ROWS_EACH, 1], F32, name="zeros")
+        nc.vector.memset(zeros[:], 0.0)
+
+        def transpose_tile(raw, t):
+            words = raw[:].bitcast(F32)
+            bank = banks.tile([P, WORDS], F32, name="bank")
+            for u in range(2):
+                for g in range(PASSES):
+                    first = t * WORDS + (2 * g + u) * P
+                    nc.tensor.transpose(
+                        bank[:, (PASSES * u + g) * P : (PASSES * u + g + 1) * P],
+                        words[:, first : first + P],
+                        ident[:],
+                    )
+            return bank
+
+        v_bank = banks.tile([P, WORDS], F32, name="bank")
+        nc.tensor.transpose(v_bank[:, 0:P], v_rows[:].bitcast(F32), ident[:])
+        bias32 = []
+        for h in range(HEADS):
+            spread = consts.tile([P, 2 * WORDS], BF16, name="bias32_%d" % h)
+            v_of_h = v_bank[:, 2 * PASSES * h : 2 * PASSES * (h + 1)].bitcast(BF16)
+            nc.vector.tensor_scalar(
+                out=spread[:].rearrange("p (g r w) -> p g r w", g=PASSES, w=4),
+                in0=v_of_h.rearrange("p (g w) -> p g w", w=4).unsqueeze(2).to_broadcast([P, PASSES, P, 4]),
+                scalar1=ROOT_K,
+                scalar2=None,
+                op0=mybir.AluOpType.mult,
+            )
+            bias32.append(spread)
+
+        def quantise(grouped, pool, name):
+            codes = pool.tile([P, CHUNK_TILES * PASSES * P], U32, name=name + "_codes", align_bytes=64)
+            scales = pool.tile([P, CHUNK_TILES * PASSES * P], U8, name=name + "_scales", align_bytes=64)
+            nc.vector.quantize_mx(out=codes[:].bitcast(FP8X4), scales=scales[:], in_=grouped[:])
+            return codes, scales
+
+        def prepare_table(h, n):
+            grouped = groupeds.tile([P, CHUNK_TILES * K], BF16, name="grouped", align_bytes=64)
+            pairs = grouped[:].bitcast(F32).rearrange("p (g j u) -> p g j u", g=PASSES, u=2)
+            for t in range(CHUNK_TILES):
+                bank = transpose_tile(raw_tables[h, n], t)
+                nc.scalar.copy(
+                    out=pairs[:, :, t * P : (t + 1) * P, :],
+                    in_=bank[:].rearrange("p (u g r) -> p g r u", u=2, g=PASSES),
+                )
+            return quantise(grouped, tables, "table%d%d" % (h, n))
+
+        def prepare_queries(b, half):
+            grouped = groupeds.tile([P, CHUNK_TILES * K], BF16, name="grouped", align_bytes=64)
+            values = grouped[:].rearrange("p (t x u e) -> p t x u e", t=CHUNK_TILES, u=2, e=2)
+            for t in range(CHUNK_TILES):
+                bank = transpose_tile(raw_queries[b, half], t)
+                nc.vector.tensor_tensor(
+                    out=values[:, t],
+                    in0=bank[:].bitcast(BF16).rearrange("p (u x e) -> p x u e", u=2, e=2),
+                    in1=bias32[b % HEADS][:].rearrange("p (x u e) -> p x u e", u=2, e=2),
+                    op=mybir.AluOpType.add,
+                )
+            return quantise(grouped, operands, "query")
+
+        def store(b, shifted, p_start, p_stop, start, stop):
+            first = b * S * T + RUN * p_start + start - T
+            nc.scalar.dma_start(
+                out=skewed_rows(out_flat, first, p_stop - p_start, stop - start),
+                in_=shifted[p_start:p_stop, start:stop],
+            )
+
+        def multiply(b, half, query, shifted):
+            codes, scales = query
+            for t in range(CHUNK_TILES):
+                row = half * CHUNK_TILES + t
+                for n in range(HALVES):
+                    table_codes, table_scales = table[b % HEADS, n]
+                    acc = sums.tile([P, N_COLS], F32, name="acc")
+                    for g in range(PASSES):
+                        rows = slice((PASSES * t + g) * P, (PASSES * t + g + 1) * P)
+                        cols = slice(g * N_COLS, (g + 1) * N_COLS)
+                        nc.tensor.matmul_mx(
+                            out=acc[:],
+                            lhsT=codes[:, rows].bitcast(FP8X4),
+                            lhsT_scale=scales[:, rows],
+                            rhs=table_codes[:, cols].bitcast(FP8X4),
+                            rhs_scale=table_scales[:, cols],
+                            start=(g == 0),
+                            stop=(g == PASSES - 1),
+                        )
+                    first = row * PADDED + 1 + n * N_COLS
+                    nc.scalar.mul(out=shifted[:, first : first + N_COLS], in_=acc[:], mul=1.0 / ROOT_K)
+                if row % 2 == 1:
+                    start = (row - 1) * T
+                    stop = (row + 1) * T if row + 1 < ROWS_EACH else RUN
+                    if row == 1:
+                        store(b, shifted, 1, 16, 0, T)
+                        store(b, shifted, 16, P, 0, T)
+                        start = T
+                    store(b, shifted, 0, P, start, stop)
+
+        table = {}
+        shifted_of = {}
+        waiting = None
+        for b in range(BATCH):
+            shifted = results.tile([P, RUN], F32, name="shifted")
+            nc.scalar.copy(
+                out=shifted[:].rearrange("p (t c) -> p t c", c=PADDED)[:, :, 0:1], in_=zeros[:]
+            )
+            shifted_of[b] = shifted
+            for half in range(HALVES):
+                query = prepare_queries(b, half)
+                if half == 0 and b < HEADS:
+                    for n in range(HALVES):
+                        table[b, n] = prepare_table(b, n)
+                if waiting is not None:
+                    multiply(*waiting)
+                waiting = (b, half, query, shifted_of[b])
+        multiply(*waiting)

@@ -22,6 +22,7 @@ CHUNK_TILES = 4
 CHUNK_ROWS = CHUNK_TILES * P
 HALVES = S // CHUNK_ROWS
 N_COLS = CHUNK_ROWS
+QUANT_WORDS = CHUNK_TILES * PASSES * P // 2
 ROWS_EACH = S // P
 PADDED = T + 1
 RUN = ROWS_EACH * PADDED
@@ -51,6 +52,7 @@ def tile_relativepositionsdpa_pa_t_kernel(tc, queries, v_bias, R, out):
         results = ctx.enter_context(tc.tile_pool(name="results", bufs=3))
         banks = ctx.enter_context(tc.psum_pool(name="banks", bufs=4))
         sums = ctx.enter_context(tc.psum_pool(name="sums", bufs=4))
+        ctx.enter_context(tc.manual_schedule())
 
         def load_chunk(rows, name):
             raw = raws.tile([P, CHUNK_TILES * K], BF16, name=name, tag="raw")
@@ -59,6 +61,10 @@ def tile_relativepositionsdpa_pa_t_kernel(tc, queries, v_bias, R, out):
 
         v_rows = consts.tile([P, 2 * P], BF16, name="v_rows")
         nc.vector.memset(v_rows[:], 0.0)
+        nc.sync.dma_start(
+            out=v_rows[0 : 2 * PASSES * HEADS, :],
+            in_=v_bias.rearrange("a h c (r w) -> (a h c r) w", w=2 * P),
+        )
 
         raw_queries = {}
         raw_tables = {}
@@ -67,11 +73,6 @@ def tile_relativepositionsdpa_pa_t_kernel(tc, queries, v_bias, R, out):
             for half in range(HALVES):
                 tiles = slice(half * CHUNK_TILES, (half + 1) * CHUNK_TILES)
                 raw_queries[b, half] = load_chunk(rows_of_b[:, tiles, :], "raw_q%d%d" % (b, half))
-                if half == 0 and b == 0:
-                    nc.sync.dma_start(
-                        out=v_rows[0 : 2 * PASSES * HEADS, :],
-                        in_=v_bias.rearrange("a h c (r w) -> (a h c r) w", w=2 * P),
-                    )
                 if half == 0 and b < HEADS:
                     for n in range(HALVES):
                         rows = R[b, n * CHUNK_ROWS : (n + 1) * CHUNK_ROWS, :]
@@ -115,7 +116,13 @@ def tile_relativepositionsdpa_pa_t_kernel(tc, queries, v_bias, R, out):
         def quantise(grouped, pool, name):
             codes = pool.tile([P, CHUNK_TILES * PASSES * P], U32, name=name + "_codes", align_bytes=64)
             scales = pool.tile([P, CHUNK_TILES * PASSES * P], U8, name=name + "_scales", align_bytes=64)
-            nc.vector.quantize_mx(out=codes[:].bitcast(FP8X4), scales=scales[:], in_=grouped[:])
+            for piece in range(2):
+                cols = slice(piece * QUANT_WORDS, (piece + 1) * QUANT_WORDS)
+                nc.vector.quantize_mx(
+                    out=codes[:, cols].bitcast(FP8X4),
+                    scales=scales[:, cols],
+                    in_=grouped[:, 4 * piece * QUANT_WORDS : 4 * (piece + 1) * QUANT_WORDS],
+                )
             return codes, scales
 
         def prepare_table(h, n):

@@ -45,7 +45,7 @@ def tile_relativepositionsdpa_pa_t_kernel(tc, queries, v_bias, R, out):
 
     with ExitStack() as ctx:
         consts = ctx.enter_context(tc.tile_pool(name="consts", bufs=1))
-        raws = ctx.enter_context(tc.tile_pool(name="raws", bufs=6))
+        raws = ctx.enter_context(tc.tile_pool(name="raws", bufs=9))
         groupeds = ctx.enter_context(tc.tile_pool(name="groupeds", bufs=3))
         tables = ctx.enter_context(tc.tile_pool(name="tables", bufs=1))
         operands = ctx.enter_context(tc.tile_pool(name="operands", bufs=3))
@@ -151,7 +151,7 @@ def tile_relativepositionsdpa_pa_t_kernel(tc, queries, v_bias, R, out):
 
         def store(b, shifted, p_start, p_stop, start, stop):
             first = b * S * T + RUN * p_start + start - T
-            nc.scalar.dma_start(
+            nc.sync.dma_start(
                 out=skewed_rows(out_flat, first, p_stop - p_start, stop - start),
                 in_=shifted[p_start:p_stop, start:stop],
             )
@@ -176,7 +176,12 @@ def tile_relativepositionsdpa_pa_t_kernel(tc, queries, v_bias, R, out):
                             stop=(g == PASSES - 1),
                         )
                     first = row * PADDED + 1 + n * N_COLS
-                    nc.scalar.mul(out=shifted[:, first : first + N_COLS], in_=acc[:], mul=1.0 / ROOT_K)
+                    nc.scalar.activation(
+                        out=shifted[:, first : first + N_COLS],
+                        in_=acc[:],
+                        func=mybir.ActivationFunctionType.Copy,
+                        scale=1.0 / ROOT_K,
+                    )
                 if row % 2 == 1:
                     start = (row - 1) * T
                     stop = (row + 1) * T if row + 1 < ROWS_EACH else RUN

@@ -26,6 +26,8 @@ QUANT_WORDS = CHUNK_TILES * PASSES * P // 2
 ROWS_EACH = S // P
 PADDED = T + 1
 RUN = ROWS_EACH * PADDED
+CHUNKS = [(b, half) for b in (0, 2, 1, 3) for half in range(HALVES)]
+TABLE1_BESIDE = {2: 0, 3: 1}
 ROOT_K = 32.0
 assert ROOT_K * ROOT_K == K
 
@@ -66,19 +68,24 @@ def tile_relativepositionsdpa_pa_t_kernel(tc, queries, v_bias, R, out):
             in_=v_bias.rearrange("a h c (r w) -> (a h c r) w", w=2 * P),
         )
 
+        def load_queries(b, half):
+            tiles = slice(half * CHUNK_TILES, (half + 1) * CHUNK_TILES)
+            rows_of_b = queries[b].rearrange("(p t) k -> p t k", t=ROWS_EACH)
+            raw_queries[b, half] = load_chunk(rows_of_b[:, tiles, :], "raw_q%d%d" % (b, half))
+
+        def load_table(h, n):
+            rows = R[h, n * CHUNK_ROWS : (n + 1) * CHUNK_ROWS, :]
+            raw_tables[h, n] = load_chunk(rows.rearrange("(t p) k -> p t k", p=P), "raw_r%d%d" % (h, n))
+
         raw_queries = {}
         raw_tables = {}
-        for b in range(BATCH):
-            rows_of_b = queries[b].rearrange("(p t) k -> p t k", t=ROWS_EACH)
-            for half in range(HALVES):
-                tiles = slice(half * CHUNK_TILES, (half + 1) * CHUNK_TILES)
-                raw_queries[b, half] = load_chunk(rows_of_b[:, tiles, :], "raw_q%d%d" % (b, half))
-                if half == 0 and b < HEADS:
-                    for n in range(HALVES):
-                        rows = R[b, n * CHUNK_ROWS : (n + 1) * CHUNK_ROWS, :]
-                        raw_tables[b, n] = load_chunk(
-                            rows.rearrange("(t p) k -> p t k", p=P), "raw_r%d%d" % (b, n)
-                        )
+        load_queries(*CHUNKS[0])
+        load_table(0, 0)
+        load_table(0, 1)
+        for i in range(1, len(CHUNKS)):
+            load_queries(*CHUNKS[i])
+            if i in TABLE1_BESIDE:
+                load_table(1, TABLE1_BESIDE[i])
 
         ident = consts.tile([P, P], F32, name="ident")
         make_identity(nc, ident[:])
@@ -156,33 +163,37 @@ def tile_relativepositionsdpa_pa_t_kernel(tc, queries, v_bias, R, out):
                 in_=shifted[p_start:p_stop, start:stop],
             )
 
-        def multiply(b, half, query, shifted):
-            codes, scales = query
-            for t in range(CHUNK_TILES):
+        def multiply(i, groups):
+            b, half = CHUNKS[i]
+            codes, scales = query[i]
+            shifted = shifted_of[b]
+            for t, n in groups:
                 row = half * CHUNK_TILES + t
-                for n in range(HALVES):
-                    table_codes, table_scales = table[b % HEADS, n]
-                    acc = sums.tile([P, N_COLS], F32, name="acc")
-                    for g in range(PASSES):
-                        rows = slice((PASSES * t + g) * P, (PASSES * t + g + 1) * P)
-                        cols = slice(g * N_COLS, (g + 1) * N_COLS)
-                        nc.tensor.matmul_mx(
-                            out=acc[:],
-                            lhsT=codes[:, rows].bitcast(FP8X4),
-                            lhsT_scale=scales[:, rows],
-                            rhs=table_codes[:, cols].bitcast(FP8X4),
-                            rhs_scale=table_scales[:, cols],
-                            start=(g == 0),
-                            stop=(g == PASSES - 1),
-                        )
-                    first = row * PADDED + 1 + n * N_COLS
-                    nc.scalar.activation(
-                        out=shifted[:, first : first + N_COLS],
-                        in_=acc[:],
-                        func=mybir.ActivationFunctionType.Copy,
-                        scale=1.0 / ROOT_K,
+                table_codes, table_scales = table[b % HEADS, n]
+                acc = sums.tile([P, N_COLS], F32, name="acc")
+                for g in range(PASSES):
+                    rows = slice((PASSES * t + g) * P, (PASSES * t + g + 1) * P)
+                    cols = slice(g * N_COLS, (g + 1) * N_COLS)
+                    nc.tensor.matmul_mx(
+                        out=acc[:],
+                        lhsT=codes[:, rows].bitcast(FP8X4),
+                        lhsT_scale=scales[:, rows],
+                        rhs=table_codes[:, cols].bitcast(FP8X4),
+                        rhs_scale=table_scales[:, cols],
+                        start=(g == 0),
+                        stop=(g == PASSES - 1),
                     )
-                if row % 2 == 1:
+                first = row * PADDED + 1 + n * N_COLS
+                result = shifted[:, first : first + N_COLS]
+                if n == 1 and t >= 2:
+                    nc.vector.tensor_scalar(
+                        out=result, in0=acc[:], scalar1=1.0 / ROOT_K, scalar2=None, op0=mybir.AluOpType.mult
+                    )
+                else:
+                    nc.scalar.activation(
+                        out=result, in_=acc[:], func=mybir.ActivationFunctionType.Copy, scale=1.0 / ROOT_K
+                    )
+                if n == HALVES - 1 and row % 2 == 1:
                     start = (row - 1) * T
                     stop = (row + 1) * T if row + 1 < ROWS_EACH else RUN
                     if row == 1:
@@ -192,20 +203,32 @@ def tile_relativepositionsdpa_pa_t_kernel(tc, queries, v_bias, R, out):
                     store(b, shifted, 0, P, start, stop)
 
         table = {}
+        query = {}
         shifted_of = {}
-        waiting = None
-        for b in range(BATCH):
+
+        def open_result(b):
             shifted = results.tile([P, RUN], F32, name="shifted")
             nc.scalar.copy(
                 out=shifted[:].rearrange("p (t c) -> p t c", c=PADDED)[:, :, 0:1], in_=zeros[:]
             )
             shifted_of[b] = shifted
-            for half in range(HALVES):
-                query = prepare_queries(b, half)
-                if half == 0 and b < HEADS:
-                    for n in range(HALVES):
-                        table[b, n] = prepare_table(b, n)
-                if waiting is not None:
-                    multiply(*waiting)
-                waiting = (b, half, query, shifted_of[b])
-        multiply(*waiting)
+
+        query[0] = prepare_queries(*CHUNKS[0])
+        for n in range(HALVES):
+            table[0, n] = prepare_table(0, n)
+        for i in range(len(CHUNKS)):
+            b, half = CHUNKS[i]
+            if half == 0:
+                open_result(b)
+            if i == 0:
+                groups = [(t, n) for n in range(HALVES) for t in range(CHUNK_TILES)]
+            else:
+                groups = [(t, n) for t in range(CHUNK_TILES) for n in range(HALVES)]
+                if i + 1 < len(CHUNKS):
+                    query[i + 1] = prepare_queries(*CHUNKS[i + 1])
+            multiply(i, groups[: len(groups) // 2])
+            if i == 0:
+                query[1] = prepare_queries(*CHUNKS[1])
+            if i in TABLE1_BESIDE:
+                table[1, TABLE1_BESIDE[i]] = prepare_table(1, TABLE1_BESIDE[i])
+            multiply(i, groups[len(groups) // 2 :])

@@ -75,7 +75,7 @@ def tile_relativepositionsdpa_pa_t_kernel(tc, queries, v_bias, R, out):
 
         def load_table(h, n):
             rows = R[h, n * CHUNK_ROWS : (n + 1) * CHUNK_ROWS, :]
-            raw_tables[h, n] = load_chunk(rows.rearrange("(t p) k -> p t k", p=P), "raw_r%d%d" % (h, n))
+            raw_tables[h, n] = load_chunk(rows.rearrange("(p t) k -> p t k", t=CHUNK_TILES), "raw_r%d%d" % (h, n))
 
         raw_queries = {}
         raw_tables = {}
@@ -184,14 +184,15 @@ def tile_relativepositionsdpa_pa_t_kernel(tc, queries, v_bias, R, out):
                         stop=(g == PASSES - 1),
                     )
                 first = row * PADDED + 1 + n * N_COLS
-                result = shifted[:, first : first + N_COLS]
+                result = shifted[:, first : first + N_COLS].rearrange("p (w t) -> p w t", t=CHUNK_TILES)
+                product = acc[:].rearrange("p (t w) -> p w t", t=CHUNK_TILES)
                 if n == 1 and t >= 2:
                     nc.vector.tensor_scalar(
-                        out=result, in0=acc[:], scalar1=1.0 / ROOT_K, scalar2=None, op0=mybir.AluOpType.mult
+                        out=result, in0=product, scalar1=1.0 / ROOT_K, scalar2=None, op0=mybir.AluOpType.mult
                     )
                 else:
                     nc.scalar.activation(
-                        out=result, in_=acc[:], func=mybir.ActivationFunctionType.Copy, scale=1.0 / ROOT_K
+                        out=result, in_=product, func=mybir.ActivationFunctionType.Copy, scale=1.0 / ROOT_K
                     )
                 if n == HALVES - 1 and row % 2 == 1:
                     start = (row - 1) * T

@@ -186,14 +186,9 @@ def tile_relativepositionsdpa_pa_t_kernel(tc, queries, v_bias, R, out):
                 first = row * PADDED + 1 + n * N_COLS
                 result = shifted[:, first : first + N_COLS].rearrange("p (w t) -> p w t", t=CHUNK_TILES)
                 product = acc[:].rearrange("p (t w) -> p w t", t=CHUNK_TILES)
-                if n == 1 and t >= 2:
-                    nc.vector.tensor_scalar(
-                        out=result, in0=product, scalar1=1.0 / ROOT_K, scalar2=None, op0=mybir.AluOpType.mult
-                    )
-                else:
-                    nc.scalar.activation(
-                        out=result, in_=product, func=mybir.ActivationFunctionType.Copy, scale=1.0 / ROOT_K
-                    )
+                nc.scalar.activation(
+                    out=result, in_=product, func=mybir.ActivationFunctionType.Copy, scale=1.0 / ROOT_K
+                )
                 if n == HALVES - 1 and row % 2 == 1:
                     start = (row - 1) * T
                     stop = (row + 1) * T if row + 1 < ROWS_EACH else RUN

@@ -28,6 +28,8 @@ PADDED = T + 1
 RUN = ROWS_EACH * PADDED
 CHUNKS = [(b, half) for b in (0, 2, 1, 3) for half in range(HALVES)]
 TABLE1_BESIDE = {2: 0, 3: 1}
+FIRST_LOAD = "raw_q%d%d" % CHUNKS[0]
+WARM_UP = 5
 ROOT_K = 32.0
 assert ROOT_K * ROOT_K == K
 
@@ -56,34 +58,43 @@ def tile_relativepositionsdpa_pa_t_kernel(tc, queries, v_bias, R, out):
         sums = ctx.enter_context(tc.psum_pool(name="sums", bufs=4))
         ctx.enter_context(tc.manual_schedule())
 
-        def load_chunk(rows, name):
-            raw = raws.tile([P, CHUNK_TILES * K], BF16, name=name, tag="raw")
-            nc.sync.dma_start(out=raw[:].rearrange("p (t k) -> p t k", t=CHUNK_TILES), in_=rows)
-            return raw
-
         v_rows = consts.tile([P, 2 * P], BF16, name="v_rows")
         nc.vector.memset(v_rows[:], 0.0)
-        nc.sync.dma_start(
-            out=v_rows[0 : 2 * PASSES * HEADS, :],
-            in_=v_bias.rearrange("a h c (r w) -> (a h c r) w", w=2 * P),
-        )
 
-        def load_queries(b, half):
+        def load_bias():
+            nc.sync.dma_start(
+                out=v_rows[0 : 2 * PASSES * HEADS, :],
+                in_=v_bias.rearrange("a h c (r w) -> (a h c r) w", w=2 * P),
+            )
+
+        def load_chunk(rows, name, pieces):
+            raw = raws.tile([P, CHUNK_TILES * K], BF16, name=name, tag="raw")
+            raw_rows = raw[:].rearrange("p (t k) -> p t k", t=CHUNK_TILES)
+            for piece in range(pieces):
+                tiles = slice(piece * CHUNK_TILES // pieces, (piece + 1) * CHUNK_TILES // pieces)
+                nc.sync.dma_start(out=raw_rows[:, tiles, :], in_=rows[:, tiles, :])
+                if piece == 0 and name == FIRST_LOAD:
+                    load_bias()
+            return raw
+
+        def load_queries(b, half, pieces=1):
             tiles = slice(half * CHUNK_TILES, (half + 1) * CHUNK_TILES)
             rows_of_b = queries[b].rearrange("(p t) k -> p t k", t=ROWS_EACH)
-            raw_queries[b, half] = load_chunk(rows_of_b[:, tiles, :], "raw_q%d%d" % (b, half))
+            raw_queries[b, half] = load_chunk(rows_of_b[:, tiles, :], "raw_q%d%d" % (b, half), pieces)
 
-        def load_table(h, n):
+        def load_table(h, n, pieces=1):
             rows = R[h, n * CHUNK_ROWS : (n + 1) * CHUNK_ROWS, :]
-            raw_tables[h, n] = load_chunk(rows.rearrange("(p t) k -> p t k", t=CHUNK_TILES), "raw_r%d%d" % (h, n))
+            raw_tables[h, n] = load_chunk(
+                rows.rearrange("(p t) k -> p t k", t=CHUNK_TILES), "raw_r%d%d" % (h, n), pieces
+            )
 
         raw_queries = {}
         raw_tables = {}
-        load_queries(*CHUNKS[0])
-        load_table(0, 0)
-        load_table(0, 1)
+        load_queries(*CHUNKS[0], pieces=2)
+        load_table(0, 0, pieces=2)
+        load_table(0, 1, pieces=2)
         for i in range(1, len(CHUNKS)):
-            load_queries(*CHUNKS[i])
+            load_queries(*CHUNKS[i], pieces=2 if i == 1 else 1)
             if i in TABLE1_BESIDE:
                 load_table(1, TABLE1_BESIDE[i])
 
@@ -91,6 +102,18 @@ def tile_relativepositionsdpa_pa_t_kernel(tc, queries, v_bias, R, out):
         make_identity(nc, ident[:])
         zeros = consts.tile([P, ROWS_EACH, 1], F32, name="zeros")
         nc.vector.memset(zeros[:], 0.0)
+
+        idle_operand = consts.tile([P, N_COLS], BF16, name="idle_operand")
+        nc.vector.memset(idle_operand[:], 0.0)
+
+        def keep_busy(count):
+            unread = sums.tile([P, N_COLS], F32, name="unread", tag="acc")
+            for repeat in range(count):
+                nc.tensor.matmul(
+                    unread[:], lhsT=idle_operand[:, 0:P], rhs=idle_operand[:], start=True, stop=True
+                )
+
+        keep_busy(WARM_UP)
 
         def transpose_tile(raw, t):
             words = raw[:].bitcast(F32)
@@ -105,19 +128,22 @@ def tile_relativepositionsdpa_pa_t_kernel(tc, queries, v_bias, R, out):
                     )
             return bank
 
-        v_bank = banks.tile([P, WORDS], F32, name="bank")
+        v_bank = sums.tile([P, WORDS], F32, name="v_bank", tag="acc")
         nc.tensor.transpose(v_bank[:, 0:P], v_rows[:].bitcast(F32), ident[:])
         bias32 = []
         for h in range(HEADS):
             spread = consts.tile([P, 2 * WORDS], BF16, name="bias32_%d" % h)
             v_of_h = v_bank[:, 2 * PASSES * h : 2 * PASSES * (h + 1)].bitcast(BF16)
-            nc.vector.tensor_scalar(
-                out=spread[:].rearrange("p (g r w) -> p g r w", g=PASSES, w=4),
-                in0=v_of_h.rearrange("p (g w) -> p g w", w=4).unsqueeze(2).to_broadcast([P, PASSES, P, 4]),
-                scalar1=ROOT_K,
-                scalar2=None,
-                op0=mybir.AluOpType.mult,
-            )
+            to = spread[:].rearrange("p (g r w) -> p g r w", g=PASSES, w=4)
+            of = v_of_h.rearrange("p (g w) -> p g w", w=4).unsqueeze(2).to_broadcast([P, PASSES, P, 4])
+            if h == CHUNKS[0][0] % HEADS:
+                nc.vector.tensor_scalar(
+                    out=to, in0=of, scalar1=ROOT_K, scalar2=None, op0=mybir.AluOpType.mult
+                )
+            else:
+                nc.scalar.activation(
+                    out=to, in_=of, func=mybir.ActivationFunctionType.Copy, scale=ROOT_K
+                )
             bias32.append(spread)
 
         def quantise(grouped, pool, name):
@@ -170,7 +196,7 @@ def tile_relativepositionsdpa_pa_t_kernel(tc, queries, v_bias, R, out):
             for t, n in groups:
                 row = half * CHUNK_TILES + t
                 table_codes, table_scales = table[b % HEADS, n]
-                acc = sums.tile([P, N_COLS], F32, name="acc")
+                acc = sums.tile([P, N_COLS], F32, name="acc", tag="acc")
                 for g in range(PASSES):
                     rows = slice((PASSES * t + g) * P, (PASSES * t + g + 1) * P)
                     cols = slice(g * N_COLS, (g + 1) * N_COLS)
@@ -211,7 +237,9 @@ def tile_relativepositionsdpa_pa_t_kernel(tc, queries, v_bias, R, out):
 
         query[0] = prepare_queries(*CHUNKS[0])
         for n in range(HALVES):
+            keep_busy(1)
             table[0, n] = prepare_table(0, n)
+        keep_busy(1)
         for i in range(len(CHUNKS)):
             b, half = CHUNKS[i]
             if half == 0:

@@ -26,9 +26,11 @@ QUANT_WORDS = CHUNK_TILES * PASSES * P // 2
 ROWS_EACH = S // P
 PADDED = T + 1
 RUN = ROWS_EACH * PADDED
-CHUNKS = [(b, half) for b in (0, 2, 1, 3) for half in range(HALVES)]
-TABLE1_BESIDE = {2: 0, 3: 1}
-FIRST_LOAD = "raw_q%d%d" % CHUNKS[0]
+BATCHES = (1, 3, 0, 2)
+CHUNKS = [(b, half) for b in BATCHES for half in range(HALVES)]
+FIRST_HEAD = BATCHES[0] % HEADS
+SECOND_HEAD = BATCHES[-1] % HEADS
+SECOND_BESIDE = {2: 0, 3: 1}
 WARM_UP = 5
 ROOT_K = 32.0
 assert ROOT_K * ROOT_K == K
@@ -67,36 +69,30 @@ def tile_relativepositionsdpa_pa_t_kernel(tc, queries, v_bias, R, out):
                 in_=v_bias.rearrange("a h c (r w) -> (a h c r) w", w=2 * P),
             )
 
-        def load_chunk(rows, name, pieces):
+        def load_chunk(rows, name):
             raw = raws.tile([P, CHUNK_TILES * K], BF16, name=name, tag="raw")
-            raw_rows = raw[:].rearrange("p (t k) -> p t k", t=CHUNK_TILES)
-            for piece in range(pieces):
-                tiles = slice(piece * CHUNK_TILES // pieces, (piece + 1) * CHUNK_TILES // pieces)
-                nc.sync.dma_start(out=raw_rows[:, tiles, :], in_=rows[:, tiles, :])
-                if piece == 0 and name == FIRST_LOAD:
-                    load_bias()
+            nc.sync.dma_start(out=raw[:].rearrange("p (t k) -> p t k", t=CHUNK_TILES), in_=rows)
             return raw
 
-        def load_queries(b, half, pieces=1):
+        def load_queries(b, half):
             tiles = slice(half * CHUNK_TILES, (half + 1) * CHUNK_TILES)
             rows_of_b = queries[b].rearrange("(p t) k -> p t k", t=ROWS_EACH)
-            raw_queries[b, half] = load_chunk(rows_of_b[:, tiles, :], "raw_q%d%d" % (b, half), pieces)
+            raw_queries[b, half] = load_chunk(rows_of_b[:, tiles, :], "raw_q%d%d" % (b, half))
 
-        def load_table(h, n, pieces=1):
+        def load_table(h, n):
             rows = R[h, n * CHUNK_ROWS : (n + 1) * CHUNK_ROWS, :]
-            raw_tables[h, n] = load_chunk(
-                rows.rearrange("(p t) k -> p t k", t=CHUNK_TILES), "raw_r%d%d" % (h, n), pieces
-            )
+            raw_tables[h, n] = load_chunk(rows.rearrange("(p t) k -> p t k", t=CHUNK_TILES), "raw_r%d%d" % (h, n))
 
         raw_queries = {}
         raw_tables = {}
-        load_queries(*CHUNKS[0], pieces=2)
-        load_table(0, 0, pieces=2)
-        load_table(0, 1, pieces=2)
+        load_queries(*CHUNKS[0])
+        load_bias()
+        load_table(FIRST_HEAD, 0)
+        load_table(FIRST_HEAD, 1)
         for i in range(1, len(CHUNKS)):
-            load_queries(*CHUNKS[i], pieces=2 if i == 1 else 1)
-            if i in TABLE1_BESIDE:
-                load_table(1, TABLE1_BESIDE[i])
+            load_queries(*CHUNKS[i])
+            if i in SECOND_BESIDE:
+                load_table(SECOND_HEAD, SECOND_BESIDE[i])
 
         ident = consts.tile([P, P], F32, name="ident")
         make_identity(nc, ident[:])
@@ -130,13 +126,13 @@ def tile_relativepositionsdpa_pa_t_kernel(tc, queries, v_bias, R, out):
 
         v_bank = sums.tile([P, WORDS], F32, name="v_bank", tag="acc")
         nc.tensor.transpose(v_bank[:, 0:P], v_rows[:].bitcast(F32), ident[:])
-        bias32 = []
-        for h in range(HEADS):
+        bias32 = {}
+        for h in (FIRST_HEAD, SECOND_HEAD):
             spread = consts.tile([P, 2 * WORDS], BF16, name="bias32_%d" % h)
             v_of_h = v_bank[:, 2 * PASSES * h : 2 * PASSES * (h + 1)].bitcast(BF16)
             to = spread[:].rearrange("p (g r w) -> p g r w", g=PASSES, w=4)
             of = v_of_h.rearrange("p (g w) -> p g w", w=4).unsqueeze(2).to_broadcast([P, PASSES, P, 4])
-            if h == CHUNKS[0][0] % HEADS:
+            if h == FIRST_HEAD:
                 nc.vector.tensor_scalar(
                     out=to, in0=of, scalar1=ROOT_K, scalar2=None, op0=mybir.AluOpType.mult
                 )
@@ -144,7 +140,7 @@ def tile_relativepositionsdpa_pa_t_kernel(tc, queries, v_bias, R, out):
                 nc.scalar.activation(
                     out=to, in_=of, func=mybir.ActivationFunctionType.Copy, scale=ROOT_K
                 )
-            bias32.append(spread)
+            bias32[h] = spread
 
         def quantise(grouped, pool, name):
             codes = pool.tile([P, CHUNK_TILES * PASSES * P], U32, name=name + "_codes", align_bytes=64)
@@ -218,7 +214,7 @@ def tile_relativepositionsdpa_pa_t_kernel(tc, queries, v_bias, R, out):
                 if n == HALVES - 1 and row % 2 == 1:
                     start = (row - 1) * T
                     stop = (row + 1) * T if row + 1 < ROWS_EACH else RUN
-                    if row == 1:
+                    if row == 1 and b - 1 not in BATCHES[i // HALVES + 1 :]:
                         store(b, shifted, 1, 16, 0, T)
                         store(b, shifted, 16, P, 0, T)
                         start = T
@@ -238,7 +234,7 @@ def tile_relativepositionsdpa_pa_t_kernel(tc, queries, v_bias, R, out):
         query[0] = prepare_queries(*CHUNKS[0])
         for n in range(HALVES):
             keep_busy(1)
-            table[0, n] = prepare_table(0, n)
+            table[FIRST_HEAD, n] = prepare_table(FIRST_HEAD, n)
         keep_busy(1)
         for i in range(len(CHUNKS)):
             b, half = CHUNKS[i]
@@ -253,6 +249,7 @@ def tile_relativepositionsdpa_pa_t_kernel(tc, queries, v_bias, R, out):
             multiply(i, groups[: len(groups) // 2])
             if i == 0:
                 query[1] = prepare_queries(*CHUNKS[1])
-            if i in TABLE1_BESIDE:
-                table[1, TABLE1_BESIDE[i]] = prepare_table(1, TABLE1_BESIDE[i])
+            if i in SECOND_BESIDE:
+                n = SECOND_BESIDE[i]
+                table[SECOND_HEAD, n] = prepare_table(SECOND_HEAD, n)
             multiply(i, groups[len(groups) // 2 :])

from contextlib import ExitStack

import concourse.mybir as mybir
from concourse.masks import make_identity

BF16 = mybir.dt.bfloat16
F32 = mybir.dt.float32
U32 = mybir.dt.uint32
U8 = mybir.dt.uint8
FP8X4 = mybir.dt.float8_e4m3fn_x4

P = 128
HEADS = 2
BATCH = 4
S = 1024
T = 1024
K = 1024
K_PASS = 4 * P
PASSES = K // K_PASS
WORDS = K // 2
CHUNK_TILES = 4
CHUNK_ROWS = CHUNK_TILES * P
HALVES = S // CHUNK_ROWS
N_COLS = CHUNK_ROWS
QUANT_WORDS = CHUNK_TILES * PASSES * P // 2
ROWS_EACH = S // P
PADDED = T + 1
RUN = ROWS_EACH * PADDED
BATCHES = (1, 3, 0, 2)
CHUNKS = [(b, half) for b in BATCHES for half in range(HALVES)]
FIRST_HEAD = BATCHES[0] % HEADS
SECOND_HEAD = BATCHES[-1] % HEADS
SECOND_BESIDE = {2: 0, 3: 1}
WARM_UP = 5
ROOT_K = 32.0
assert ROOT_K * ROOT_K == K

FLOPS = 2 * BATCH * S * T * K
BYTES = 2 * BATCH * S * K + 2 * HEADS * K + 2 * HEADS * T * K + 4 * BATCH * S * T


def skewed_rows(out_flat, first, rows, width):
    lead = min(first, RUN - width)
    window = out_flat[first - lead : first - lead + rows * RUN]
    return window.rearrange("(r x) -> r x", x=RUN)[:, lead : lead + width]


def tile_relativepositionsdpa_pa_t_kernel(tc, queries, v_bias, R, out):
    nc = tc.nc
    out_flat = out.rearrange("b s t -> (b s t)")

    with ExitStack() as ctx:
        consts = ctx.enter_context(tc.tile_pool(name="consts", bufs=1))
        raws = ctx.enter_context(tc.tile_pool(name="raws", bufs=9))
        groupeds = ctx.enter_context(tc.tile_pool(name="groupeds", bufs=3))
        tables = ctx.enter_context(tc.tile_pool(name="tables", bufs=1))
        operands = ctx.enter_context(tc.tile_pool(name="operands", bufs=3))
        results = ctx.enter_context(tc.tile_pool(name="results", bufs=3))
        banks = ctx.enter_context(tc.psum_pool(name="banks", bufs=4))
        sums = ctx.enter_context(tc.psum_pool(name="sums", bufs=4))
        ctx.enter_context(tc.manual_schedule())

        v_rows = consts.tile([P, 2 * P], BF16, name="v_rows")
        nc.vector.memset(v_rows[:], 0.0)

        def load_bias():
            nc.sync.dma_start(
                out=v_rows[0 : 2 * PASSES * HEADS, :],
                in_=v_bias.rearrange("a h c (r w) -> (a h c r) w", w=2 * P),
            )

        def load_chunk(rows, name):
            raw = raws.tile([P, CHUNK_TILES * K], BF16, name=name, tag="raw")
            nc.sync.dma_start(out=raw[:].rearrange("p (t k) -> p t k", t=CHUNK_TILES), in_=rows)
            return raw

        def load_queries(b, half):
            tiles = slice(half * CHUNK_TILES, (half + 1) * CHUNK_TILES)
            rows_of_b = queries[b].rearrange("(p t) k -> p t k", t=ROWS_EACH)
            raw_queries[b, half] = load_chunk(rows_of_b[:, tiles, :], "raw_q%d%d" % (b, half))

        def load_table(h, n):
            rows = R[h, n * CHUNK_ROWS : (n + 1) * CHUNK_ROWS, :]
            raw_tables[h, n] = load_chunk(rows.rearrange("(p t) k -> p t k", t=CHUNK_TILES), "raw_r%d%d" % (h, n))

        raw_queries = {}
        raw_tables = {}
        load_queries(*CHUNKS[0])
        load_bias()
        load_table(FIRST_HEAD, 0)
        load_table(FIRST_HEAD, 1)
        for i in range(1, len(CHUNKS)):
            load_queries(*CHUNKS[i])
            if i in SECOND_BESIDE:
                load_table(SECOND_HEAD, SECOND_BESIDE[i])

        ident = consts.tile([P, P], F32, name="ident")
        make_identity(nc, ident[:])
        zeros = consts.tile([P, ROWS_EACH, 1], F32, name="zeros")
        nc.vector.memset(zeros[:], 0.0)

        idle_operand = consts.tile([P, N_COLS], BF16, name="idle_operand")
        nc.vector.memset(idle_operand[:], 0.0)

        def keep_busy(count):
            unread = sums.tile([P, N_COLS], F32, name="unread", tag="acc")
            for repeat in range(count):
                nc.tensor.matmul(
                    unread[:], lhsT=idle_operand[:, 0:P], rhs=idle_operand[:], start=True, stop=True
                )

        keep_busy(WARM_UP)

        def transpose_tile(raw, t):
            words = raw[:].bitcast(F32)
            bank = banks.tile([P, WORDS], F32, name="bank")
            for u in range(2):
                for g in range(PASSES):
                    first = t * WORDS + (2 * g + u) * P
                    nc.tensor.transpose(
                        bank[:, (PASSES * u + g) * P : (PASSES * u + g + 1) * P],
                        words[:, first : first + P],
                        ident[:],
                    )
            return bank

        v_bank = sums.tile([P, WORDS], F32, name="v_bank", tag="acc")
        nc.tensor.transpose(v_bank[:, 0:P], v_rows[:].bitcast(F32), ident[:])
        bias32 = {}
        for h in (FIRST_HEAD, SECOND_HEAD):
            spread = consts.tile([P, 2 * WORDS], BF16, name="bias32_%d" % h)
            v_of_h = v_bank[:, 2 * PASSES * h : 2 * PASSES * (h + 1)].bitcast(BF16)
            to = spread[:].rearrange("p (g r w) -> p g r w", g=PASSES, w=4)
            of = v_of_h.rearrange("p (g w) -> p g w", w=4).unsqueeze(2).to_broadcast([P, PASSES, P, 4])
            if h == FIRST_HEAD:
                nc.vector.tensor_scalar(
                    out=to, in0=of, scalar1=ROOT_K, scalar2=None, op0=mybir.AluOpType.mult
                )
            else:
                nc.scalar.activation(
                    out=to, in_=of, func=mybir.ActivationFunctionType.Copy, scale=ROOT_K
                )
            bias32[h] = spread

        def quantise(grouped, pool, name):
            codes = pool.tile([P, CHUNK_TILES * PASSES * P], U32, name=name + "_codes", align_bytes=64)
            scales = pool.tile([P, CHUNK_TILES * PASSES * P], U8, name=name + "_scales", align_bytes=64)
            for piece in range(2):
                cols = slice(piece * QUANT_WORDS, (piece + 1) * QUANT_WORDS)
                nc.vector.quantize_mx(
                    out=codes[:, cols].bitcast(FP8X4),
                    scales=scales[:, cols],
                    in_=grouped[:, 4 * piece * QUANT_WORDS : 4 * (piece + 1) * QUANT_WORDS],
                )
            return codes, scales

        def prepare_table(h, n):
            grouped = groupeds.tile([P, CHUNK_TILES * K], BF16, name="grouped", align_bytes=64)
            pairs = grouped[:].bitcast(F32).rearrange("p (g j u) -> p g j u", g=PASSES, u=2)
            for t in range(CHUNK_TILES):
                bank = transpose_tile(raw_tables[h, n], t)
                nc.scalar.copy(
                    out=pairs[:, :, t * P : (t + 1) * P, :],
                    in_=bank[:].rearrange("p (u g r) -> p g r u", u=2, g=PASSES),
                )
            return quantise(grouped, tables, "table%d%d" % (h, n))

        def prepare_queries(b, half):
            grouped = groupeds.tile([P, CHUNK_TILES * K], BF16, name="grouped", align_bytes=64)
            values = grouped[:].rearrange("p (t x u e) -> p t x u e", t=CHUNK_TILES, u=2, e=2)
            for t in range(CHUNK_TILES):
                bank = transpose_tile(raw_queries[b, half], t)
                nc.vector.tensor_tensor(
                    out=values[:, t],
                    in0=bank[:].bitcast(BF16).rearrange("p (u x e) -> p x u e", u=2, e=2),
                    in1=bias32[b % HEADS][:].rearrange("p (x u e) -> p x u e", u=2, e=2),
                    op=mybir.AluOpType.add,
                )
            return quantise(grouped, operands, "query")

        def store(b, shifted, p_start, p_stop, start, stop):
            first = b * S * T + RUN * p_start + start - T
            nc.sync.dma_start(
                out=skewed_rows(out_flat, first, p_stop - p_start, stop - start),
                in_=shifted[p_start:p_stop, start:stop],
            )

        def multiply(i, groups):
            b, half = CHUNKS[i]
            codes, scales = query[i]
            shifted = shifted_of[b]
            for t, n in groups:
                row = half * CHUNK_TILES + t
                table_codes, table_scales = table[b % HEADS, n]
                acc = sums.tile([P, N_COLS], F32, name="acc", tag="acc")
                for g in range(PASSES):
                    rows = slice((PASSES * t + g) * P, (PASSES * t + g + 1) * P)
                    cols = slice(g * N_COLS, (g + 1) * N_COLS)
                    nc.tensor.matmul_mx(
                        out=acc[:],
                        lhsT=codes[:, rows].bitcast(FP8X4),
                        lhsT_scale=scales[:, rows],
                        rhs=table_codes[:, cols].bitcast(FP8X4),
                        rhs_scale=table_scales[:, cols],
                        start=(g == 0),
                        stop=(g == PASSES - 1),
                    )
                first = row * PADDED + 1 + n * N_COLS
                result = shifted[:, first : first + N_COLS].rearrange("p (w t) -> p w t", t=CHUNK_TILES)
                product = acc[:].rearrange("p (t w) -> p w t", t=CHUNK_TILES)
                nc.scalar.activation(
                    out=result, in_=product, func=mybir.ActivationFunctionType.Copy, scale=1.0 / ROOT_K
                )
                if n == HALVES - 1 and row % 2 == 1:
                    start = (row - 1) * T
                    stop = (row + 1) * T if row + 1 < ROWS_EACH else RUN
                    if row == 1 and b - 1 not in BATCHES[i // HALVES + 1 :]:
                        store(b, shifted, 1, 16, 0, T)
                        store(b, shifted, 16, P, 0, T)
                        start = T
                    store(b, shifted, 0, P, start, stop)

        table = {}
        query = {}
        shifted_of = {}

        def open_result(b):
            shifted = results.tile([P, RUN], F32, name="shifted")
            nc.scalar.copy(
                out=shifted[:].rearrange("p (t c) -> p t c", c=PADDED)[:, :, 0:1], in_=zeros[:]
            )
            shifted_of[b] = shifted

        query[0] = prepare_queries(*CHUNKS[0])
        for n in range(HALVES):
            keep_busy(1)
            table[FIRST_HEAD, n] = prepare_table(FIRST_HEAD, n)
        keep_busy(1)
        for i in range(len(CHUNKS)):
            b, half = CHUNKS[i]
            if half == 0:
                open_result(b)
            if i == 0:
                groups = [(t, n) for n in range(HALVES) for t in range(CHUNK_TILES)]
            else:
                groups = [(t, n) for t in range(CHUNK_TILES) for n in range(HALVES)]
                if i + 1 < len(CHUNKS):
                    query[i + 1] = prepare_queries(*CHUNKS[i + 1])
            multiply(i, groups[: len(groups) // 2])
            if i == 0:
                query[1] = prepare_queries(*CHUNKS[1])
            if i in SECOND_BESIDE:
                n = SECOND_BESIDE[i]
                table[SECOND_HEAD, n] = prepare_table(SECOND_HEAD, n)
            multiply(i, groups[len(groups) // 2 :])
